import numpy as np
import ml_dtypes


def mxq(x, axis, fmt="e4m3"):
    dtype, down = {"e4m3": (ml_dtypes.float8_e4m3fn, 7), "e5m2": (ml_dtypes.float8_e5m2, 14)}[fmt]
    v = np.moveaxis(np.asarray(x, np.float32).astype(ml_dtypes.bfloat16).astype(np.float64), axis, -1)
    blocks = v.reshape(v.shape[:-1] + (-1, 32))
    amax = np.abs(blocks).max(-1, keepdims=True)
    byte = np.maximum(np.where(amax > 0, np.frexp(amax)[1] - 1 + 127, 0) - down, 1)
    scale = np.exp2(byte - 127.0)
    codes = (blocks / scale).astype(np.float32).astype(dtype).astype(np.float64)
    return np.moveaxis((codes * scale).reshape(v.shape), -1, axis)


WIDE = False


def mx_kscale(k):
    if not WIDE:
        return np.ones(k)
    levels = np.array([10, -10, 5, -5, 0])
    a = np.random.permutation(np.resize(levels, k // 512 * 4)).reshape(k // 512, 4)
    idx = np.arange(k)
    return np.exp2(a[idx // 512, idx % 128 // 32])


BF16 = ml_dtypes.bfloat16


def bf(x):
    return np.asarray(x, np.float32).astype(BF16)


def f64(x):
    return np.asarray(x).astype(np.float64)


E2M1 = np.array([0.0, 0.5, 1.0, 1.5, 2.0, 3.0, 4.0, 6.0, -0.0, -0.5, -1.0, -1.5, -2.0, -3.0, -4.0, -6.0])


def pack_weight(w, fmt):
    k, n = w.shape
    w = f64(bf(w)).reshape(k // 32, 32, n)
    amax = np.abs(w).max(1)
    if fmt == "e4m3":
        byte = np.frexp(amax)[1] - 1 + 127 - 7
    else:
        mant, ex = np.frexp(amax / 6.0)
        byte = np.where(mant > 0.5, ex, ex - 1) + 127
    byte = np.clip(np.where(amax > 0, byte, 1), 1, 254)
    scaled = (w * np.exp2(127.0 - byte)[:, None, :]).reshape(k, n).astype(np.float32)
    by_word = np.ascontiguousarray(scaled.reshape(k // 512, 128, 4, n).transpose(0, 1, 3, 2))
    if fmt == "e4m3":
        words = by_word.astype(ml_dtypes.float8_e4m3fn).view(np.uint8)
    else:
        c = by_word.astype(ml_dtypes.float4_e2m1fn).view(np.uint8) & 0xF
        words = c[..., 0::2] | (c[..., 1::2] << 4)
    return np.ascontiguousarray(words), np.ascontiguousarray(byte.astype(np.uint8).reshape(k // 512, 16, n))


def unpack_weight(words, scales, fmt):
    g, p, n, _ = words.shape
    if fmt == "e4m3":
        vals = np.ascontiguousarray(words).view(ml_dtypes.float8_e4m3fn).astype(np.float64)
    else:
        nib = np.empty((g, p, n, 4), np.uint8)
        nib[..., 0::2] = words & 0xF
        nib[..., 1::2] = words >> 4
        vals = E2M1[nib]
    vals = vals * np.repeat(np.exp2(scales.astype(np.float64) - 127.0), 8, axis=1)[..., None]
    return vals.transpose(0, 1, 3, 2).reshape(g * 512, n)

def pack4(w):
    words, scales = pack_weight(w, "e2m1")
    return words.reshape(words.shape[0], 128, -1), scales


def unpack4(words, scales):
    return unpack_weight(words.reshape(words.shape[0], 128, -1, 2), scales, "e2m1")


B, T, C, H = 4, 1024, 512, 4
HD = C // H


def rotary_pos_emb(v):
    exponents = f64(np.arange(0, HD, 2)[: HD // 2] // HD)
    freqs = 1.0 / np.power(1000.0, exponents)
    theta = f64(np.arange(T))[:, None] * freqs[None, :]
    cos = np.cos(theta)[None, :, None, :]
    sin = np.sin(theta)[None, :, None, :]
    vr = v.reshape(B, T, H, HD // 2, 2)
    v0, v1 = vr[..., 0], vr[..., 1]
    out = np.stack([v0 * cos - v1 * sin, v0 * sin + v1 * cos], axis=-1)
    return out.reshape(B, T, H, HD)


def setup_inputs():
    s = mx_kscale(C)
    x = bf(np.random.standard_normal((B, T, C)) * s)
    wq = np.random.standard_normal((C, C)) / np.sqrt(C) / s[None, :]
    wk = np.random.standard_normal((C, C)) / np.sqrt(C) / s[None, :]
    wq_words, wq_scales = pack4(np.ascontiguousarray(wq.T))
    wk_words, wk_scales = pack4(np.ascontiguousarray(wk.T))
    return {"x": x,
            "wq_words": wq_words, "wq_scales": wq_scales,
            "wk_words": wk_words, "wk_scales": wk_scales}


def reference(x, wq_words, wq_scales, wk_words, wk_scales):
    xm = mxq(f64(x), 2, "e4m3")
    q = (xm @ unpack4(wq_words, wq_scales)).reshape(B, T, H, HD)
    k = (xm @ unpack4(wk_words, wk_scales)).reshape(B, T, H, HD)
    return rotary_pos_emb(q), rotary_pos_emb(k)

@@ -1,0 +1,275 @@
+import math
+from contextlib import ExitStack
+
+import concourse.mybir as mybir
+from concourse.masks import make_identity
+
+F32 = mybir.dt.float32
+BF16 = mybir.dt.bfloat16
+I32 = mybir.dt.int32
+U32 = mybir.dt.uint32
+U8 = mybir.dt.uint8
+FP8X4 = mybir.dt.float8_e4m3fn_x4
+FP4X4 = mybir.dt.float4_e2m1fn_x4
+ALU = mybir.AluOpType
+ACT = mybir.ActivationFunctionType
+
+P = 128
+BATCH = 4
+SEQ = 1024
+CH = 512
+PAIRS = CH // 2
+WORDS = CH // 2
+POS_PER_PARTITION = SEQ // P
+GROUP_TILES = 4
+GROUP_TOKENS = GROUP_TILES * P
+GROUPS = BATCH * SEQ // GROUP_TOKENS
+GROUPS_PER_BATCH = SEQ // GROUP_TOKENS
+BANK_TILES = 2
+BANK_TOKENS = BANK_TILES * P
+GROUP_BANKS = GROUP_TILES // BANK_TILES
+STORE_TILES = 2
+SCALAR_COPY_EVERY = 4
+
+FLOPS = 2 * BATCH * SEQ * CH * 2 * CH
+
+PI_HIGH = 3.140625
+PI_MIDDLE = 0.0009675025939941406
+PI_LOW = 1.5099580252808664e-07
+HALF_PI_HIGH = 1.5707963705062866
+HALF_PI_LOW = -4.371138828673793e-08
+ROUND_MAGIC = 12582912.0
+
+
+def build_rotation_tables(nc, pool):
+    shape = [P, POS_PER_PARTITION]
+    position_int = pool.tile(shape, I32)
+    nc.gpsimd.iota(
+        position_int[:], pattern=[[1, POS_PER_PARTITION]], base=0, channel_multiplier=POS_PER_PARTITION
+    )
+    position = pool.tile(shape, F32)
+    nc.vector.tensor_copy(out=position[:], in_=position_int[:])
+
+    shifted = pool.tile(shape, F32)
+    nc.vector.tensor_scalar(
+        out=shifted[:], in0=position[:], scalar1=1.0 / math.pi, scalar2=ROUND_MAGIC, op0=ALU.mult, op1=ALU.add
+    )
+    half_turns = pool.tile(shape, F32)
+    nc.vector.tensor_scalar(
+        out=half_turns[:], in0=shifted[:], scalar1=ROUND_MAGIC, scalar2=None, op0=ALU.subtract
+    )
+    odd = pool.tile(shape, I32)
+    nc.vector.tensor_scalar(
+        out=odd[:], in0=shifted[:].bitcast(I32), scalar1=1, scalar2=None, op0=ALU.bitwise_and
+    )
+    sign = pool.tile(shape, F32)
+    nc.vector.tensor_scalar(out=sign[:], in0=odd[:], scalar1=-2.0, scalar2=1.0, op0=ALU.mult, op1=ALU.add)
+
+    rest_a = pool.tile(shape, F32)
+    nc.vector.scalar_tensor_tensor(
+        out=rest_a[:], in0=half_turns[:], scalar=-PI_HIGH, in1=position[:], op0=ALU.mult, op1=ALU.add
+    )
+    rest_b = pool.tile(shape, F32)
+    nc.vector.scalar_tensor_tensor(
+        out=rest_b[:], in0=half_turns[:], scalar=-PI_MIDDLE, in1=rest_a[:], op0=ALU.mult, op1=ALU.add
+    )
+    rest = pool.tile(shape, F32)
+    nc.vector.scalar_tensor_tensor(
+        out=rest[:], in0=half_turns[:], scalar=-PI_LOW, in1=rest_b[:], op0=ALU.mult, op1=ALU.add
+    )
+    rest_plus = pool.tile(shape, F32)
+    nc.vector.tensor_scalar(
+        out=rest_plus[:], in0=rest[:], scalar1=HALF_PI_HIGH, scalar2=HALF_PI_LOW, op0=ALU.add, op1=ALU.add
+    )
+
+    sin_rest = pool.tile(shape, F32)
+    nc.scalar.activation(out=sin_rest[:], in_=rest[:], func=ACT.Sin)
+    cos_rest = pool.tile(shape, F32)
+    nc.scalar.activation(out=cos_rest[:], in_=rest_plus[:], func=ACT.Sin)
+
+    cos = pool.tile(shape, F32)
+    nc.vector.tensor_tensor(out=cos[:], in0=cos_rest[:], in1=sign[:], op=ALU.mult)
+    sin = pool.tile(shape, F32)
+    nc.vector.tensor_tensor(out=sin[:], in0=sin_rest[:], in1=sign[:], op=ALU.mult)
+    neg_sin = pool.tile(shape, F32)
+    nc.vector.tensor_scalar(out=neg_sin[:], in0=sin[:], scalar1=-1.0, scalar2=None, op0=ALU.mult)
+    one_over_cos = pool.tile(shape, F32)
+    nc.vector.reciprocal(out=one_over_cos[:], in_=cos[:])
+    tan = pool.tile(shape, F32)
+    nc.vector.tensor_tensor(out=tan[:], in0=sin[:], in1=one_over_cos[:], op=ALU.mult)
+    neg_tan = pool.tile(shape, F32)
+    nc.vector.tensor_scalar(out=neg_tan[:], in0=tan[:], scalar1=-1.0, scalar2=None, op0=ALU.mult)
+    return cos, sin, neg_sin, tan, neg_tan
+
+
+def tile_attention_pa_t_kernel(tc, x, wq_words, wq_scales, wk_words, wk_scales, out_0, out_1):
+    nc = tc.nc
+    weights = ((wq_words, wq_scales), (wk_words, wk_scales))
+    outputs = (out_0, out_1)
+
+    with ExitStack() as ctx:
+        consts = ctx.enter_context(tc.tile_pool(name="consts", bufs=1))
+        x_pool = ctx.enter_context(tc.tile_pool(name="x", bufs=GROUPS))
+        quant_pool = ctx.enter_context(tc.tile_pool(name="quant", bufs=3))
+        cross_pool = ctx.enter_context(tc.tile_pool(name="cross", bufs=6))
+        slow_pool = ctx.enter_context(tc.tile_pool(name="slow", bufs=2))
+        rot_pool = ctx.enter_context(tc.tile_pool(name="rot", bufs=3))
+        psum_x = ctx.enter_context(tc.psum_pool(name="psum_x", bufs=2))
+        psum_mm = ctx.enter_context(tc.psum_pool(name="psum_mm", bufs=6))
+
+        def group_rows(tensor_of_batch, g):
+            first = (g % GROUPS_PER_BATCH) * GROUP_TILES
+            return tensor_of_batch[:, first : first + GROUP_TILES, :]
+
+        x_tiles = []
+
+        def load_x(g):
+            x_group = x_pool.tile([P, GROUP_TILES, CH], BF16)
+            by_partition = x[g // GROUPS_PER_BATCH].rearrange("(p t) c -> p t c", t=POS_PER_PARTITION)
+            nc.sync.dma_start(out=x_group[:], in_=group_rows(by_partition, g))
+            x_tiles.append(x_group)
+
+        w_words = consts.tile([P, 2, 2 * CH], U8, align_bytes=64)
+        w_planes = consts.tile([P, 2, CH], U8, align_bytes=64)
+        nc.vector.memset(w_planes[:].bitcast(I32), 0)
+
+        load_x(0)
+        for which, (words, scales) in enumerate(weights):
+            for quadrant in range(4):
+                nc.sync.dma_start(
+                    out=w_planes[32 * quadrant : 32 * quadrant + 4, which, :].bitcast(I32),
+                    in_=scales[0, 4 * quadrant : 4 * quadrant + 4, :].bitcast(I32),
+                )
+            nc.sync.dma_start(out=w_words[:, which, :].bitcast(I32), in_=words[0].bitcast(I32))
+        for g in range(1, GROUPS):
+            load_x(g)
+
+        identity = consts.tile([P, P], F32)
+        make_identity(nc, identity[:])
+        cos, sin, neg_sin, tan, neg_tan = build_rotation_tables(nc, consts)
+
+        quantised = {}
+
+        def quantise_group(g):
+            x_words = x_tiles[g][:].bitcast(F32)
+            codes = quant_pool.tile([P, GROUP_TOKENS], U32, align_bytes=64)
+            plane = quant_pool.tile([P, GROUP_TOKENS], U8, align_bytes=64)
+            for bank in range(GROUP_BANKS):
+                transposed = psum_x.tile([P, BANK_TILES, 2, P], F32)
+                for j in range(BANK_TILES):
+                    for u in range(2):
+                        nc.tensor.transpose(
+                            transposed[:, j, u, :],
+                            x_words[:, bank * BANK_TILES + j, u:WORDS:2],
+                            identity[:],
+                        )
+                grouped = quant_pool.tile([P, BANK_TOKENS, 4], BF16, align_bytes=64)
+                copy_index = g * GROUP_BANKS + bank
+                on_scalar = copy_index % SCALAR_COPY_EVERY == SCALAR_COPY_EVERY - 1
+                copy_out = nc.scalar.copy if on_scalar else nc.vector.tensor_copy
+                copy_out(
+                    out=grouped[:].bitcast(F32).rearrange("p (j m) u -> p j m u", j=BANK_TILES),
+                    in_=transposed[:].rearrange("p j u m -> p j m u"),
+                )
+                tokens = slice(bank * BANK_TOKENS, (bank + 1) * BANK_TOKENS)
+                nc.vector.quantize_mx(
+                    out=codes[:, tokens].bitcast(FP8X4),
+                    scales=plane[:, tokens],
+                    in_=grouped[:].rearrange("p m t -> p (m t)"),
+                )
+            quantised[g] = (codes, plane)
+
+        def project(codes, plane, j, which):
+            tokens = slice(j * P, (j + 1) * P)
+            acc = psum_mm.tile([P, CH], F32)
+            nc.tensor.matmul_mx(
+                out=acc[:],
+                lhsT=codes[:, tokens].bitcast(FP8X4),
+                lhsT_scale=plane[:, tokens],
+                rhs=w_words[:, which, :].bitcast(FP4X4),
+                rhs_scale=w_planes[:, which, :],
+                start=True,
+                stop=True,
+            )
+            return acc
+
+        rotated_groups = {}
+
+        def rotate_tile_0(g):
+            codes, plane = quantised[g]
+            t = (g % GROUPS_PER_BATCH) * GROUP_TILES
+            rotated = rot_pool.tile([P, 2, GROUP_TILES, CH], F32)
+            rotated_groups[g] = rotated
+            scaled = slow_pool.tile([P, 2, PAIRS, 2], F32)
+            for which in range(2):
+                acc = project(codes, plane, 0, which)
+                nc.scalar.activation(
+                    out=scaled[:, which, :, :].rearrange("p i two -> p (i two)"),
+                    in_=acc[:],
+                    func=ACT.Copy,
+                    scale=cos[:, t : t + 1],
+                )
+            slow_cross = slow_pool.tile([P, 2, 2, PAIRS], F32)
+            nc.gpsimd.tensor_scalar(
+                out=slow_cross[:, :, 0, :],
+                in0=scaled[:, :, :, 1],
+                scalar1=neg_tan[:, t : t + 1],
+                scalar2=0.0,
+                op0=ALU.mult,
+                op1=ALU.add,
+            )
+            nc.gpsimd.tensor_scalar(
+                out=slow_cross[:, :, 1, :],
+                in0=scaled[:, :, :, 0],
+                scalar1=tan[:, t : t + 1],
+                scalar2=0.0,
+                op0=ALU.mult,
+                op1=ALU.add,
+            )
+            nc.gpsimd.tensor_tensor(
+                out=rotated[:, :, 0, :].rearrange("p w (i two) -> p w i two", two=2),
+                in0=scaled[:],
+                in1=slow_cross[:].rearrange("p w two i -> p w i two"),
+                op=ALU.add,
+            )
+
+        def rotate_other_tiles(g):
+            codes, plane = quantised[g]
+            rotated = rotated_groups[g]
+            first_t = (g % GROUPS_PER_BATCH) * GROUP_TILES
+            for which in range(2):
+                by_partition = outputs[which][g // GROUPS_PER_BATCH].rearrange(
+                    "(p t) h d -> p t (h d)", t=POS_PER_PARTITION
+                )
+                for j in range(1, GROUP_TILES):
+                    t = first_t + j
+                    acc = project(codes, plane, j, which)
+                    pairs = acc[:].rearrange("p (i two) -> p i two", two=2)
+                    cross = cross_pool.tile([P, 2, PAIRS], F32)
+                    nc.scalar.activation(
+                        out=cross[:, 0, :], in_=pairs[:, :, 1], func=ACT.Copy, scale=neg_sin[:, t : t + 1]
+                    )
+                    nc.scalar.activation(
+                        out=cross[:, 1, :], in_=pairs[:, :, 0], func=ACT.Copy, scale=sin[:, t : t + 1]
+                    )
+                    nc.vector.scalar_tensor_tensor(
+                        out=rotated[:, which, j, :].rearrange("p (i two) -> p i two", two=2),
+                        in0=pairs,
+                        scalar=cos[:, t : t + 1],
+                        in1=cross[:].rearrange("p two i -> p i two"),
+                        op0=ALU.mult,
+                        op1=ALU.add,
+                    )
+                    if (j + 1) % STORE_TILES == 0:
+                        done = slice(j + 1 - STORE_TILES, j + 1)
+                        nc.sync.dma_start(
+                            out=group_rows(by_partition, g)[:, done, :], in_=rotated[:, which, done, :]
+                        )
+
+        quantise_group(0)
+        rotate_tile_0(0)
+        for g in range(GROUPS):
+            if g + 1 < GROUPS:
+                quantise_group(g + 1)
+                rotate_tile_0(g + 1)
+            rotate_other_tiles(g)

@@ -29,7 +29,7 @@ BANK_TILES = 2
 BANK_TOKENS = BANK_TILES * P
 GROUP_BANKS = GROUP_TILES // BANK_TILES
 STORE_TILES = 2
-SCALAR_COPY_EVERY = 4
+SCALAR_COPY_EVERY = 2
 
 FLOPS = 2 * BATCH * SEQ * CH * 2 * CH
 
@@ -93,13 +93,7 @@ def build_rotation_tables(nc, pool):
     nc.vector.tensor_tensor(out=sin[:], in0=sin_rest[:], in1=sign[:], op=ALU.mult)
     neg_sin = pool.tile(shape, F32)
     nc.vector.tensor_scalar(out=neg_sin[:], in0=sin[:], scalar1=-1.0, scalar2=None, op0=ALU.mult)
-    one_over_cos = pool.tile(shape, F32)
-    nc.vector.reciprocal(out=one_over_cos[:], in_=cos[:])
-    tan = pool.tile(shape, F32)
-    nc.vector.tensor_tensor(out=tan[:], in0=sin[:], in1=one_over_cos[:], op=ALU.mult)
-    neg_tan = pool.tile(shape, F32)
-    nc.vector.tensor_scalar(out=neg_tan[:], in0=tan[:], scalar1=-1.0, scalar2=None, op0=ALU.mult)
-    return cos, sin, neg_sin, tan, neg_tan
+    return cos, sin, neg_sin
 
 
 def tile_attention_pa_t_kernel(tc, x, wq_words, wq_scales, wk_words, wk_scales, out_0, out_1):
@@ -112,7 +106,6 @@ def tile_attention_pa_t_kernel(tc, x, wq_words, wq_scales, wk_words, wk_scales, 
         x_pool = ctx.enter_context(tc.tile_pool(name="x", bufs=GROUPS))
         quant_pool = ctx.enter_context(tc.tile_pool(name="quant", bufs=3))
         cross_pool = ctx.enter_context(tc.tile_pool(name="cross", bufs=6))
-        slow_pool = ctx.enter_context(tc.tile_pool(name="slow", bufs=2))
         rot_pool = ctx.enter_context(tc.tile_pool(name="rot", bufs=3))
         psum_x = ctx.enter_context(tc.psum_pool(name="psum_x", bufs=2))
         psum_mm = ctx.enter_context(tc.psum_pool(name="psum_mm", bufs=6))
@@ -146,7 +139,7 @@ def tile_attention_pa_t_kernel(tc, x, wq_words, wq_scales, wk_words, wk_scales, 
 
         identity = consts.tile([P, P], F32)
         make_identity(nc, identity[:])
-        cos, sin, neg_sin, tan, neg_tan = build_rotation_tables(nc, consts)
+        cos, sin, neg_sin = build_rotation_tables(nc, consts)
 
         quantised = {}
 
@@ -193,55 +186,15 @@ def tile_attention_pa_t_kernel(tc, x, wq_words, wq_scales, wk_words, wk_scales, 
             )
             return acc
 
-        rotated_groups = {}
-
-        def rotate_tile_0(g):
+        def project_and_rotate_group(g):
             codes, plane = quantised[g]
-            t = (g % GROUPS_PER_BATCH) * GROUP_TILES
             rotated = rot_pool.tile([P, 2, GROUP_TILES, CH], F32)
-            rotated_groups[g] = rotated
-            scaled = slow_pool.tile([P, 2, PAIRS, 2], F32)
-            for which in range(2):
-                acc = project(codes, plane, 0, which)
-                nc.scalar.activation(
-                    out=scaled[:, which, :, :].rearrange("p i two -> p (i two)"),
-                    in_=acc[:],
-                    func=ACT.Copy,
-                    scale=cos[:, t : t + 1],
-                )
-            slow_cross = slow_pool.tile([P, 2, 2, PAIRS], F32)
-            nc.gpsimd.tensor_scalar(
-                out=slow_cross[:, :, 0, :],
-                in0=scaled[:, :, :, 1],
-                scalar1=neg_tan[:, t : t + 1],
-                scalar2=0.0,
-                op0=ALU.mult,
-                op1=ALU.add,
-            )
-            nc.gpsimd.tensor_scalar(
-                out=slow_cross[:, :, 1, :],
-                in0=scaled[:, :, :, 0],
-                scalar1=tan[:, t : t + 1],
-                scalar2=0.0,
-                op0=ALU.mult,
-                op1=ALU.add,
-            )
-            nc.gpsimd.tensor_tensor(
-                out=rotated[:, :, 0, :].rearrange("p w (i two) -> p w i two", two=2),
-                in0=scaled[:],
-                in1=slow_cross[:].rearrange("p w two i -> p w i two"),
-                op=ALU.add,
-            )
-
-        def rotate_other_tiles(g):
-            codes, plane = quantised[g]
-            rotated = rotated_groups[g]
             first_t = (g % GROUPS_PER_BATCH) * GROUP_TILES
             for which in range(2):
                 by_partition = outputs[which][g // GROUPS_PER_BATCH].rearrange(
                     "(p t) h d -> p t (h d)", t=POS_PER_PARTITION
                 )
-                for j in range(1, GROUP_TILES):
+                for j in range(GROUP_TILES):
                     t = first_t + j
                     acc = project(codes, plane, j, which)
                     pairs = acc[:].rearrange("p (i two) -> p i two", two=2)
@@ -267,9 +220,7 @@ def tile_attention_pa_t_kernel(tc, x, wq_words, wq_scales, wk_words, wk_scales, 
                         )
 
         quantise_group(0)
-        rotate_tile_0(0)
         for g in range(GROUPS):
             if g + 1 < GROUPS:
                 quantise_group(g + 1)
-                rotate_tile_0(g + 1)
-            rotate_other_tiles(g)
+            project_and_rotate_group(g)

@@ -29,7 +29,6 @@ BANK_TILES = 2
 BANK_TOKENS = BANK_TILES * P
 GROUP_BANKS = GROUP_TILES // BANK_TILES
 STORE_TILES = 2
-SCALAR_COPY_EVERY = 2
 
 FLOPS = 2 * BATCH * SEQ * CH * 2 * CH
 
@@ -106,7 +105,7 @@ def tile_attention_pa_t_kernel(tc, x, wq_words, wq_scales, wk_words, wk_scales, 
         x_pool = ctx.enter_context(tc.tile_pool(name="x", bufs=GROUPS))
         quant_pool = ctx.enter_context(tc.tile_pool(name="quant", bufs=3))
         cross_pool = ctx.enter_context(tc.tile_pool(name="cross", bufs=6))
-        rot_pool = ctx.enter_context(tc.tile_pool(name="rot", bufs=3))
+        rot_pool = ctx.enter_context(tc.tile_pool(name="rot", bufs=6))
         psum_x = ctx.enter_context(tc.psum_pool(name="psum_x", bufs=2))
         psum_mm = ctx.enter_context(tc.psum_pool(name="psum_mm", bufs=6))
 
@@ -145,6 +144,7 @@ def tile_attention_pa_t_kernel(tc, x, wq_words, wq_scales, wk_words, wk_scales, 
 
         def quantise_group(g):
             x_words = x_tiles[g][:].bitcast(F32)
+            grouped = quant_pool.tile([P, GROUP_TOKENS, 4], BF16, align_bytes=64)
             codes = quant_pool.tile([P, GROUP_TOKENS], U32, align_bytes=64)
             plane = quant_pool.tile([P, GROUP_TOKENS], U8, align_bytes=64)
             for bank in range(GROUP_BANKS):
@@ -156,19 +156,18 @@ def tile_attention_pa_t_kernel(tc, x, wq_words, wq_scales, wk_words, wk_scales, 
                             x_words[:, bank * BANK_TILES + j, u:WORDS:2],
                             identity[:],
                         )
-                grouped = quant_pool.tile([P, BANK_TOKENS, 4], BF16, align_bytes=64)
-                copy_index = g * GROUP_BANKS + bank
-                on_scalar = copy_index % SCALAR_COPY_EVERY == SCALAR_COPY_EVERY - 1
-                copy_out = nc.scalar.copy if on_scalar else nc.vector.tensor_copy
+                tokens = slice(bank * BANK_TOKENS, (bank + 1) * BANK_TOKENS)
+                copy_out = nc.scalar.copy if bank == 0 else nc.vector.tensor_copy
                 copy_out(
-                    out=grouped[:].bitcast(F32).rearrange("p (j m) u -> p j m u", j=BANK_TILES),
+                    out=grouped[:, tokens, :].bitcast(F32).rearrange("p (j m) u -> p j m u", j=BANK_TILES),
                     in_=transposed[:].rearrange("p j u m -> p j m u"),
                 )
+            for bank in range(GROUP_BANKS):
                 tokens = slice(bank * BANK_TOKENS, (bank + 1) * BANK_TOKENS)
                 nc.vector.quantize_mx(
                     out=codes[:, tokens].bitcast(FP8X4),
                     scales=plane[:, tokens],
-                    in_=grouped[:].rearrange("p m t -> p (m t)"),
+                    in_=grouped[:, tokens, :].rearrange("p m t -> p (m t)"),
                 )
             quantised[g] = (codes, plane)
 
@@ -186,41 +185,42 @@ def tile_attention_pa_t_kernel(tc, x, wq_words, wq_scales, wk_words, wk_scales, 
             )
             return acc
 
-        def project_and_rotate_group(g):
+        def project_and_rotate(g, which):
             codes, plane = quantised[g]
-            rotated = rot_pool.tile([P, 2, GROUP_TILES, CH], F32)
+            rotated = rot_pool.tile([P, GROUP_TILES, CH], F32)
             first_t = (g % GROUPS_PER_BATCH) * GROUP_TILES
-            for which in range(2):
-                by_partition = outputs[which][g // GROUPS_PER_BATCH].rearrange(
-                    "(p t) h d -> p t (h d)", t=POS_PER_PARTITION
+            by_partition = outputs[which][g // GROUPS_PER_BATCH].rearrange(
+                "(p t) h d -> p t (h d)", t=POS_PER_PARTITION
+            )
+            for j in range(GROUP_TILES):
+                t = first_t + j
+                acc = project(codes, plane, j, which)
+                pairs = acc[:].rearrange("p (i two) -> p i two", two=2)
+                cross = cross_pool.tile([P, 2, PAIRS], F32)
+                nc.scalar.activation(
+                    out=cross[:, 0, :], in_=pairs[:, :, 1], func=ACT.Copy, scale=neg_sin[:, t : t + 1]
                 )
-                for j in range(GROUP_TILES):
-                    t = first_t + j
-                    acc = project(codes, plane, j, which)
-                    pairs = acc[:].rearrange("p (i two) -> p i two", two=2)
-                    cross = cross_pool.tile([P, 2, PAIRS], F32)
-                    nc.scalar.activation(
-                        out=cross[:, 0, :], in_=pairs[:, :, 1], func=ACT.Copy, scale=neg_sin[:, t : t + 1]
+                nc.scalar.activation(
+                    out=cross[:, 1, :], in_=pairs[:, :, 0], func=ACT.Copy, scale=sin[:, t : t + 1]
+                )
+                nc.vector.scalar_tensor_tensor(
+                    out=rotated[:, j, :].rearrange("p (i two) -> p i two", two=2),
+                    in0=pairs,
+                    scalar=cos[:, t : t + 1],
+                    in1=cross[:].rearrange("p two i -> p i two"),
+                    op0=ALU.mult,
+                    op1=ALU.add,
+                )
+                if (j + 1) % STORE_TILES == 0:
+                    done = slice(j + 1 - STORE_TILES, j + 1)
+                    nc.sync.dma_start(
+                        out=group_rows(by_partition, g)[:, done, :], in_=rotated[:, done, :]
                     )
-                    nc.scalar.activation(
-                        out=cross[:, 1, :], in_=pairs[:, :, 0], func=ACT.Copy, scale=sin[:, t : t + 1]
-                    )
-                    nc.vector.scalar_tensor_tensor(
-                        out=rotated[:, which, j, :].rearrange("p (i two) -> p i two", two=2),
-                        in0=pairs,
-                        scalar=cos[:, t : t + 1],
-                        in1=cross[:].rearrange("p two i -> p i two"),
-                        op0=ALU.mult,
-                        op1=ALU.add,
-                    )
-                    if (j + 1) % STORE_TILES == 0:
-                        done = slice(j + 1 - STORE_TILES, j + 1)
-                        nc.sync.dma_start(
-                            out=group_rows(by_partition, g)[:, done, :], in_=rotated[:, which, done, :]
-                        )
 
-        quantise_group(0)
-        for g in range(GROUPS):
-            if g + 1 < GROUPS:
-                quantise_group(g + 1)
-            project_and_rotate_group(g)
+        with tc.manual_schedule():
+            quantise_group(0)
+            for g in range(GROUPS):
+                project_and_rotate(g, 0)
+                if g + 1 < GROUPS:
+                    quantise_group(g + 1)
+                project_and_rotate(g, 1)

@@ -29,6 +29,7 @@ BANK_TILES = 2
 BANK_TOKENS = BANK_TILES * P
 GROUP_BANKS = GROUP_TILES // BANK_TILES
 STORE_TILES = 2
+AHEAD = 2
 
 FLOPS = 2 * BATCH * SEQ * CH * 2 * CH
 
@@ -103,7 +104,7 @@ def tile_attention_pa_t_kernel(tc, x, wq_words, wq_scales, wk_words, wk_scales, 
     with ExitStack() as ctx:
         consts = ctx.enter_context(tc.tile_pool(name="consts", bufs=1))
         x_pool = ctx.enter_context(tc.tile_pool(name="x", bufs=GROUPS))
-        quant_pool = ctx.enter_context(tc.tile_pool(name="quant", bufs=3))
+        quant_pool = ctx.enter_context(tc.tile_pool(name="quant", bufs=AHEAD + 2))
         cross_pool = ctx.enter_context(tc.tile_pool(name="cross", bufs=6))
         rot_pool = ctx.enter_context(tc.tile_pool(name="rot", bufs=6))
         psum_x = ctx.enter_context(tc.psum_pool(name="psum_x", bufs=2))
@@ -218,9 +219,10 @@ def tile_attention_pa_t_kernel(tc, x, wq_words, wq_scales, wk_words, wk_scales, 
                     )
 
         with tc.manual_schedule():
-            quantise_group(0)
+            for g in range(AHEAD):
+                quantise_group(g)
             for g in range(GROUPS):
                 project_and_rotate(g, 0)
-                if g + 1 < GROUPS:
-                    quantise_group(g + 1)
+                if g + AHEAD < GROUPS:
+                    quantise_group(g + AHEAD)
                 project_and_rotate(g, 1)

@@ -28,7 +28,8 @@ GROUPS_PER_BATCH = SEQ // GROUP_TOKENS
 BANK_TILES = 2
 BANK_TOKENS = BANK_TILES * P
 GROUP_BANKS = GROUP_TILES // BANK_TILES
-STORE_TILES = 2
+STORE_TILES = 4
+LAST_STORE_TILES = 2
 AHEAD = 2
 
 FLOPS = 2 * BATCH * SEQ * CH * 2 * CH
@@ -212,8 +213,9 @@ def tile_attention_pa_t_kernel(tc, x, wq_words, wq_scales, wk_words, wk_scales, 
                     op0=ALU.mult,
                     op1=ALU.add,
                 )
-                if (j + 1) % STORE_TILES == 0:
-                    done = slice(j + 1 - STORE_TILES, j + 1)
+                store_tiles = LAST_STORE_TILES if g == GROUPS - 1 else STORE_TILES
+                if (j + 1) % store_tiles == 0:
+                    done = slice(j + 1 - store_tiles, j + 1)
                     nc.sync.dma_start(
                         out=group_rows(by_partition, g)[:, done, :], in_=rotated[:, done, :]
                     )

@@ -117,17 +117,19 @@ def tile_attention_pa_t_kernel(tc, x, wq_words, wq_scales, wk_words, wk_scales, 
 
         x_tiles = []
 
-        def load_x(g):
+        def load_x(g, pieces):
             x_group = x_pool.tile([P, GROUP_TILES, CH], BF16)
             by_partition = x[g // GROUPS_PER_BATCH].rearrange("(p t) c -> p t c", t=POS_PER_PARTITION)
-            nc.sync.dma_start(out=x_group[:], in_=group_rows(by_partition, g))
+            for piece in range(pieces):
+                tiles = slice(piece * GROUP_TILES // pieces, (piece + 1) * GROUP_TILES // pieces)
+                nc.sync.dma_start(out=x_group[:, tiles, :], in_=group_rows(by_partition, g)[:, tiles, :])
             x_tiles.append(x_group)
 
         w_words = consts.tile([P, 2, 2 * CH], U8, align_bytes=64)
         w_planes = consts.tile([P, 2, CH], U8, align_bytes=64)
         nc.vector.memset(w_planes[:].bitcast(I32), 0)
 
-        load_x(0)
+        load_x(0, GROUP_BANKS)
         for which, (words, scales) in enumerate(weights):
             for quadrant in range(4):
                 nc.sync.dma_start(
@@ -135,8 +137,11 @@ def tile_attention_pa_t_kernel(tc, x, wq_words, wq_scales, wk_words, wk_scales, 
                     in_=scales[0, 4 * quadrant : 4 * quadrant + 4, :].bitcast(I32),
                 )
             nc.sync.dma_start(out=w_words[:, which, :].bitcast(I32), in_=words[0].bitcast(I32))
-        for g in range(1, GROUPS):
-            load_x(g)
+            if which == 0:
+                for g in range(1, AHEAD + 1):
+                    load_x(g, 1)
+        for g in range(AHEAD + 1, GROUPS):
+            load_x(g, 1)
 
         identity = consts.tile([P, P], F32)
         make_identity(nc, identity[:])

@@ -164,7 +164,8 @@ def tile_attention_pa_t_kernel(tc, x, wq_words, wq_scales, wk_words, wk_scales, 
                             identity[:],
                         )
                 tokens = slice(bank * BANK_TOKENS, (bank + 1) * BANK_TOKENS)
-                copy_out = nc.scalar.copy if bank == 0 else nc.vector.tensor_copy
+                scalar_takes_both = g >= AHEAD and g % 2 == 1
+                copy_out = nc.scalar.copy if bank == 0 or scalar_takes_both else nc.vector.tensor_copy
                 copy_out(
                     out=grouped[:, tokens, :].bitcast(F32).rearrange("p (j m) u -> p j m u", j=BANK_TILES),
                     in_=transposed[:].rearrange("p j u m -> p j m u"),

@@ -31,6 +31,7 @@ GROUP_BANKS = GROUP_TILES // BANK_TILES
 STORE_TILES = 4
 LAST_STORE_TILES = 2
 AHEAD = 2
+WARM_UP_MATMULS = 4
 
 FLOPS = 2 * BATCH * SEQ * CH * 2 * CH
 
@@ -125,6 +126,9 @@ def tile_attention_pa_t_kernel(tc, x, wq_words, wq_scales, wk_words, wk_scales, 
                 nc.sync.dma_start(out=x_group[:, tiles, :], in_=group_rows(by_partition, g)[:, tiles, :])
             x_tiles.append(x_group)
 
+        zero_words = consts.tile([P, CH // 2], F32)
+        nc.vector.memset(zero_words[:], 0.0)
+        zeros = zero_words[:].bitcast(BF16)
         w_words = consts.tile([P, 2, 2 * CH], U8, align_bytes=64)
         w_planes = consts.tile([P, 2, CH], U8, align_bytes=64)
         nc.vector.memset(w_planes[:].bitcast(I32), 0)
@@ -227,6 +231,9 @@ def tile_attention_pa_t_kernel(tc, x, wq_words, wq_scales, wk_words, wk_scales, 
                     )
 
         with tc.manual_schedule():
+            acc = psum_mm.tile([P, CH], F32)
+            for step in range(WARM_UP_MATMULS):
+                nc.tensor.matmul(out=acc[:], lhsT=zeros[:, :P], rhs=zeros, start=True, stop=True)
             for g in range(AHEAD):
                 quantise_group(g)
             for g in range(GROUPS):

@@ -168,7 +168,7 @@ def tile_attention_pa_t_kernel(tc, x, wq_words, wq_scales, wk_words, wk_scales, 
                             identity[:],
                         )
                 tokens = slice(bank * BANK_TOKENS, (bank + 1) * BANK_TOKENS)
-                scalar_takes_both = g >= AHEAD and g % 2 == 1
+                scalar_takes_both = g >= AHEAD and g % 3 == 0
                 copy_out = nc.scalar.copy if bank == 0 or scalar_takes_both else nc.vector.tensor_copy
                 copy_out(
                     out=grouped[:, tokens, :].bitcast(F32).rearrange("p (j m) u -> p j m u", j=BANK_TILES),

@@ -95,7 +95,13 @@ def build_rotation_tables(nc, pool):
     nc.vector.tensor_tensor(out=sin[:], in0=sin_rest[:], in1=sign[:], op=ALU.mult)
     neg_sin = pool.tile(shape, F32)
     nc.vector.tensor_scalar(out=neg_sin[:], in0=sin[:], scalar1=-1.0, scalar2=None, op0=ALU.mult)
-    return cos, sin, neg_sin
+    inverse_cos = pool.tile(shape, F32)
+    nc.vector.reciprocal(out=inverse_cos[:], in_=cos[:])
+    tan = pool.tile(shape, F32)
+    nc.vector.tensor_tensor(out=tan[:], in0=sin[:], in1=inverse_cos[:], op=ALU.mult)
+    neg_tan = pool.tile(shape, F32)
+    nc.vector.tensor_scalar(out=neg_tan[:], in0=tan[:], scalar1=-1.0, scalar2=None, op0=ALU.mult)
+    return cos, sin, neg_sin, tan, neg_tan
 
 
 def tile_attention_pa_t_kernel(tc, x, wq_words, wq_scales, wk_words, wk_scales, out_0, out_1):
@@ -108,6 +114,8 @@ def tile_attention_pa_t_kernel(tc, x, wq_words, wq_scales, wk_words, wk_scales, 
         x_pool = ctx.enter_context(tc.tile_pool(name="x", bufs=GROUPS))
         quant_pool = ctx.enter_context(tc.tile_pool(name="quant", bufs=AHEAD + 2))
         cross_pool = ctx.enter_context(tc.tile_pool(name="cross", bufs=6))
+        scaled_pool = ctx.enter_context(tc.tile_pool(name="scaled", bufs=2))
+        turned_pool = ctx.enter_context(tc.tile_pool(name="turned", bufs=2))
         rot_pool = ctx.enter_context(tc.tile_pool(name="rot", bufs=6))
         psum_x = ctx.enter_context(tc.psum_pool(name="psum_x", bufs=2))
         psum_mm = ctx.enter_context(tc.psum_pool(name="psum_mm", bufs=6))
@@ -149,7 +157,7 @@ def tile_attention_pa_t_kernel(tc, x, wq_words, wq_scales, wk_words, wk_scales, 
 
         identity = consts.tile([P, P], F32)
         make_identity(nc, identity[:])
-        cos, sin, neg_sin = build_rotation_tables(nc, consts)
+        cos, sin, neg_sin, tan, neg_tan = build_rotation_tables(nc, consts)
 
         quantised = {}
 
@@ -168,7 +176,7 @@ def tile_attention_pa_t_kernel(tc, x, wq_words, wq_scales, wk_words, wk_scales, 
                             identity[:],
                         )
                 tokens = slice(bank * BANK_TOKENS, (bank + 1) * BANK_TOKENS)
-                scalar_takes_both = g >= AHEAD and g % 3 == 0
+                scalar_takes_both = g >= AHEAD
                 copy_out = nc.scalar.copy if bank == 0 or scalar_takes_both else nc.vector.tensor_copy
                 copy_out(
                     out=grouped[:, tokens, :].bitcast(F32).rearrange("p (j m) u -> p j m u", j=BANK_TILES),
@@ -197,10 +205,34 @@ def tile_attention_pa_t_kernel(tc, x, wq_words, wq_scales, wk_words, wk_scales, 
             )
             return acc
 
+        def rotate_on_gpsimd(acc, t, out_tile):
+            scaled = scaled_pool.tile([P, CH], F32)
+            nc.vector.tensor_scalar(
+                out=scaled[:], in0=acc[:], scalar1=cos[:, t : t + 1], scalar2=None, op0=ALU.mult
+            )
+            scaled_pairs = scaled[:].rearrange("p (i two) -> p i two", two=2)
+            turned = turned_pool.tile([P, 2, PAIRS], F32)
+            for plane, factor in ((0, neg_tan), (1, tan)):
+                nc.gpsimd.tensor_scalar(
+                    out=turned[:, plane, :],
+                    in0=scaled_pairs[:, :, 1 - plane],
+                    scalar1=factor[:, t : t + 1],
+                    scalar2=0.0,
+                    op0=ALU.mult,
+                    op1=ALU.add,
+                )
+            nc.gpsimd.tensor_tensor(
+                out=out_tile.rearrange("p (i two) -> p i two", two=2),
+                in0=scaled_pairs,
+                in1=turned[:].rearrange("p two i -> p i two"),
+                op=ALU.add,
+            )
+
         def project_and_rotate(g, which):
             codes, plane = quantised[g]
             rotated = rot_pool.tile([P, GROUP_TILES, CH], F32)
             first_t = (g % GROUPS_PER_BATCH) * GROUP_TILES
+            gpsimd_weight = 1 if g + AHEAD < GROUPS else 0
             by_partition = outputs[which][g // GROUPS_PER_BATCH].rearrange(
                 "(p t) h d -> p t (h d)", t=POS_PER_PARTITION
             )
@@ -208,6 +240,9 @@ def tile_attention_pa_t_kernel(tc, x, wq_words, wq_scales, wk_words, wk_scales, 
                 t = first_t + j
                 acc = project(codes, plane, j, which)
                 pairs = acc[:].rearrange("p (i two) -> p i two", two=2)
+                if j == 0 and which == gpsimd_weight:
+                    rotate_on_gpsimd(acc, t, rotated[:, j, :])
+                    continue
                 cross = cross_pool.tile([P, 2, PAIRS], F32)
                 nc.scalar.activation(
                     out=cross[:, 0, :], in_=pairs[:, :, 1], func=ACT.Copy, scale=neg_sin[:, t : t + 1]

@@ -232,7 +232,6 @@ def tile_attention_pa_t_kernel(tc, x, wq_words, wq_scales, wk_words, wk_scales, 
             codes, plane = quantised[g]
             rotated = rot_pool.tile([P, GROUP_TILES, CH], F32)
             first_t = (g % GROUPS_PER_BATCH) * GROUP_TILES
-            gpsimd_weight = 1 if g + AHEAD < GROUPS else 0
             by_partition = outputs[which][g // GROUPS_PER_BATCH].rearrange(
                 "(p t) h d -> p t (h d)", t=POS_PER_PARTITION
             )
@@ -240,7 +239,7 @@ def tile_attention_pa_t_kernel(tc, x, wq_words, wq_scales, wk_words, wk_scales, 
                 t = first_t + j
                 acc = project(codes, plane, j, which)
                 pairs = acc[:].rearrange("p (i two) -> p i two", two=2)
-                if j == 0 and which == gpsimd_weight:
+                if j == 0 and which == 1 and g < GROUPS - 2:
                     rotate_on_gpsimd(acc, t, rotated[:, j, :])
                     continue
                 cross = cross_pool.tile([P, 2, PAIRS], F32)
@@ -258,7 +257,7 @@ def tile_attention_pa_t_kernel(tc, x, wq_words, wq_scales, wk_words, wk_scales, 
                     op0=ALU.mult,
                     op1=ALU.add,
                 )
-                store_tiles = LAST_STORE_TILES if g == GROUPS - 1 else STORE_TILES
+                store_tiles = LAST_STORE_TILES if g >= GROUPS - 2 else STORE_TILES
                 if (j + 1) % store_tiles == 0:
                     done = slice(j + 1 - store_tiles, j + 1)
                     nc.sync.dma_start(

@@ -20,11 +20,11 @@ SEQ = 1024
 CH = 512
 PAIRS = CH // 2
 WORDS = CH // 2
-POS_PER_PARTITION = SEQ // P
 GROUP_TILES = 4
 GROUP_TOKENS = GROUP_TILES * P
 GROUPS = BATCH * SEQ // GROUP_TOKENS
 GROUPS_PER_BATCH = SEQ // GROUP_TOKENS
+TABLE_COLUMNS = GROUPS_PER_BATCH * GROUP_TILES
 BANK_TILES = 2
 BANK_TOKENS = BANK_TILES * P
 GROUP_BANKS = GROUP_TILES // BANK_TILES
@@ -44,10 +44,13 @@ ROUND_MAGIC = 12582912.0
 
 
 def build_rotation_tables(nc, pool):
-    shape = [P, POS_PER_PARTITION]
+    shape = [P, TABLE_COLUMNS]
     position_int = pool.tile(shape, I32)
     nc.gpsimd.iota(
-        position_int[:], pattern=[[1, POS_PER_PARTITION]], base=0, channel_multiplier=POS_PER_PARTITION
+        position_int[:],
+        pattern=[[GROUP_TOKENS, GROUPS_PER_BATCH], [1, GROUP_TILES]],
+        base=0,
+        channel_multiplier=GROUP_TILES,
     )
     position = pool.tile(shape, F32)
     nc.vector.tensor_copy(out=position[:], in_=position_int[:])
@@ -121,14 +124,13 @@ def tile_attention_pa_t_kernel(tc, x, wq_words, wq_scales, wk_words, wk_scales, 
         psum_mm = ctx.enter_context(tc.psum_pool(name="psum_mm", bufs=6))
 
         def group_rows(tensor_of_batch, g):
-            first = (g % GROUPS_PER_BATCH) * GROUP_TILES
-            return tensor_of_batch[:, first : first + GROUP_TILES, :]
+            return tensor_of_batch[g % GROUPS_PER_BATCH]
 
         x_tiles = []
 
         def load_x(g, pieces):
             x_group = x_pool.tile([P, GROUP_TILES, CH], BF16)
-            by_partition = x[g // GROUPS_PER_BATCH].rearrange("(p t) c -> p t c", t=POS_PER_PARTITION)
+            by_partition = x[g // GROUPS_PER_BATCH].rearrange("(h p j) c -> h p j c", p=P, j=GROUP_TILES)
             for piece in range(pieces):
                 tiles = slice(piece * GROUP_TILES // pieces, (piece + 1) * GROUP_TILES // pieces)
                 nc.sync.dma_start(out=x_group[:, tiles, :], in_=group_rows(by_partition, g)[:, tiles, :])
@@ -233,7 +235,7 @@ def tile_attention_pa_t_kernel(tc, x, wq_words, wq_scales, wk_words, wk_scales, 
             rotated = rot_pool.tile([P, GROUP_TILES, CH], F32)
             first_t = (g % GROUPS_PER_BATCH) * GROUP_TILES
             by_partition = outputs[which][g // GROUPS_PER_BATCH].rearrange(
-                "(p t) h d -> p t (h d)", t=POS_PER_PARTITION
+                "(half p j) h d -> half p j (h d)", p=P, j=GROUP_TILES
             )
             for j in range(GROUP_TILES):
                 t = first_t + j

@@ -28,8 +28,7 @@ TABLE_COLUMNS = GROUPS_PER_BATCH * GROUP_TILES
 BANK_TILES = 2
 BANK_TOKENS = BANK_TILES * P
 GROUP_BANKS = GROUP_TILES // BANK_TILES
-STORE_TILES = 4
-LAST_STORE_TILES = 2
+GPSIMD_GROUPS = 5
 AHEAD = 2
 WARM_UP_MATMULS = 4
 
@@ -144,6 +143,7 @@ def tile_attention_pa_t_kernel(tc, x, wq_words, wq_scales, wk_words, wk_scales, 
         nc.vector.memset(w_planes[:].bitcast(I32), 0)
 
         load_x(0, GROUP_BANKS)
+        load_x(1, 1)
         for which, (words, scales) in enumerate(weights):
             for quadrant in range(4):
                 nc.sync.dma_start(
@@ -152,8 +152,7 @@ def tile_attention_pa_t_kernel(tc, x, wq_words, wq_scales, wk_words, wk_scales, 
                 )
             nc.sync.dma_start(out=w_words[:, which, :].bitcast(I32), in_=words[0].bitcast(I32))
             if which == 0:
-                for g in range(1, AHEAD + 1):
-                    load_x(g, 1)
+                load_x(AHEAD, 1)
         for g in range(AHEAD + 1, GROUPS):
             load_x(g, 1)
 
@@ -241,7 +240,7 @@ def tile_attention_pa_t_kernel(tc, x, wq_words, wq_scales, wk_words, wk_scales, 
                 t = first_t + j
                 acc = project(codes, plane, j, which)
                 pairs = acc[:].rearrange("p (i two) -> p i two", two=2)
-                if j == 0 and which == 1 and g < GROUPS - 2:
+                if j == 0 and which == 1 and g < GPSIMD_GROUPS:
                     rotate_on_gpsimd(acc, t, rotated[:, j, :])
                     continue
                 cross = cross_pool.tile([P, 2, PAIRS], F32)
@@ -259,12 +258,7 @@ def tile_attention_pa_t_kernel(tc, x, wq_words, wq_scales, wk_words, wk_scales, 
                     op0=ALU.mult,
                     op1=ALU.add,
                 )
-                store_tiles = LAST_STORE_TILES if g >= GROUPS - 2 else STORE_TILES
-                if (j + 1) % store_tiles == 0:
-                    done = slice(j + 1 - store_tiles, j + 1)
-                    nc.sync.dma_start(
-                        out=group_rows(by_partition, g)[:, done, :], in_=rotated[:, done, :]
-                    )
+            nc.sync.dma_start(out=group_rows(by_partition, g), in_=rotated[:])
 
         with tc.manual_schedule():
             acc = psum_mm.tile([P, CH], F32)

@@ -258,7 +258,14 @@ def tile_attention_pa_t_kernel(tc, x, wq_words, wq_scales, wk_words, wk_scales, 
                     op0=ALU.mult,
                     op1=ALU.add,
                 )
-            nc.sync.dma_start(out=group_rows(by_partition, g), in_=rotated[:])
+            first_tiles = 1 if which == 1 and g < GPSIMD_GROUPS else 0
+            nc.sync.dma_start(
+                out=group_rows(by_partition, g)[:, first_tiles:, :], in_=rotated[:, first_tiles:, :]
+            )
+            if first_tiles > 0:
+                nc.sync.dma_start(
+                    out=group_rows(by_partition, g)[:, :first_tiles, :], in_=rotated[:, :first_tiles, :]
+                )
 
         with tc.manual_schedule():
             acc = psum_mm.tile([P, CH], F32)

@@ -42,7 +42,7 @@ HALF_PI_LOW = -4.371138828673793e-08
 ROUND_MAGIC = 12582912.0
 
 
-def build_rotation_tables(nc, pool):
+def reduce_positions(nc, pool):
     shape = [P, TABLE_COLUMNS]
     position_int = pool.tile(shape, I32)
     nc.gpsimd.iota(
@@ -86,24 +86,38 @@ def build_rotation_tables(nc, pool):
         out=rest_plus[:], in0=rest[:], scalar1=HALF_PI_HIGH, scalar2=HALF_PI_LOW, op0=ALU.add, op1=ALU.add
     )
 
+    return rest, rest_plus, sign
+
+
+def take_sines(nc, pool, rest, rest_plus):
+    shape = [P, TABLE_COLUMNS]
     sin_rest = pool.tile(shape, F32)
     nc.scalar.activation(out=sin_rest[:], in_=rest[:], func=ACT.Sin)
     cos_rest = pool.tile(shape, F32)
     nc.scalar.activation(out=cos_rest[:], in_=rest_plus[:], func=ACT.Sin)
+    return sin_rest, cos_rest
 
+
+def make_tables(nc, pool, sin_rest, cos_rest, sign):
+    shape = [P, TABLE_COLUMNS]
     cos = pool.tile(shape, F32)
     nc.vector.tensor_tensor(out=cos[:], in0=cos_rest[:], in1=sign[:], op=ALU.mult)
     sin = pool.tile(shape, F32)
     nc.vector.tensor_tensor(out=sin[:], in0=sin_rest[:], in1=sign[:], op=ALU.mult)
     neg_sin = pool.tile(shape, F32)
     nc.vector.tensor_scalar(out=neg_sin[:], in0=sin[:], scalar1=-1.0, scalar2=None, op0=ALU.mult)
+    return cos, sin, neg_sin
+
+
+def make_tangents(nc, pool, cos, sin):
+    shape = [P, TABLE_COLUMNS]
     inverse_cos = pool.tile(shape, F32)
     nc.vector.reciprocal(out=inverse_cos[:], in_=cos[:])
     tan = pool.tile(shape, F32)
     nc.vector.tensor_tensor(out=tan[:], in0=sin[:], in1=inverse_cos[:], op=ALU.mult)
     neg_tan = pool.tile(shape, F32)
     nc.vector.tensor_scalar(out=neg_tan[:], in0=tan[:], scalar1=-1.0, scalar2=None, op0=ALU.mult)
-    return cos, sin, neg_sin, tan, neg_tan
+    return tan, neg_tan
 
 
 def tile_attention_pa_t_kernel(tc, x, wq_words, wq_scales, wk_words, wk_scales, out_0, out_1):
@@ -158,7 +172,6 @@ def tile_attention_pa_t_kernel(tc, x, wq_words, wq_scales, wk_words, wk_scales, 
 
         identity = consts.tile([P, P], F32)
         make_identity(nc, identity[:])
-        cos, sin, neg_sin, tan, neg_tan = build_rotation_tables(nc, consts)
 
         quantised = {}
 
@@ -271,8 +284,15 @@ def tile_attention_pa_t_kernel(tc, x, wq_words, wq_scales, wk_words, wk_scales, 
             acc = psum_mm.tile([P, CH], F32)
             for step in range(WARM_UP_MATMULS):
                 nc.tensor.matmul(out=acc[:], lhsT=zeros[:, :P], rhs=zeros, start=True, stop=True)
-            for g in range(AHEAD):
+            table_load = consts.tile([P, 1], F32)
+            nc.scalar.activation(out=table_load[:], in_=zero_words[:, :1], func=ACT.Sin)
+            rest, rest_plus, sign = reduce_positions(nc, consts)
+            quantise_group(0)
+            sin_rest, cos_rest = take_sines(nc, consts, rest, rest_plus)
+            cos, sin, neg_sin = make_tables(nc, consts, sin_rest, cos_rest, sign)
+            for g in range(1, AHEAD):
                 quantise_group(g)
+            tan, neg_tan = make_tangents(nc, consts, cos, sin)
             for g in range(GROUPS):
                 project_and_rotate(g, 0)
                 if g + AHEAD < GROUPS:

import math
from contextlib import ExitStack

import concourse.mybir as mybir
from concourse.masks import make_identity

F32 = mybir.dt.float32
BF16 = mybir.dt.bfloat16
I32 = mybir.dt.int32
U32 = mybir.dt.uint32
U8 = mybir.dt.uint8
FP8X4 = mybir.dt.float8_e4m3fn_x4
FP4X4 = mybir.dt.float4_e2m1fn_x4
ALU = mybir.AluOpType
ACT = mybir.ActivationFunctionType

P = 128
BATCH = 4
SEQ = 1024
CH = 512
PAIRS = CH // 2
WORDS = CH // 2
GROUP_TILES = 4
GROUP_TOKENS = GROUP_TILES * P
GROUPS = BATCH * SEQ // GROUP_TOKENS
GROUPS_PER_BATCH = SEQ // GROUP_TOKENS
TABLE_COLUMNS = GROUPS_PER_BATCH * GROUP_TILES
BANK_TILES = 2
BANK_TOKENS = BANK_TILES * P
GROUP_BANKS = GROUP_TILES // BANK_TILES
GPSIMD_GROUPS = 5
AHEAD = 2
WARM_UP_MATMULS = 4

FLOPS = 2 * BATCH * SEQ * CH * 2 * CH

PI_HIGH = 3.140625
PI_MIDDLE = 0.0009675025939941406
PI_LOW = 1.5099580252808664e-07
HALF_PI_HIGH = 1.5707963705062866
HALF_PI_LOW = -4.371138828673793e-08
ROUND_MAGIC = 12582912.0


def reduce_positions(nc, pool):
    shape = [P, TABLE_COLUMNS]
    position_int = pool.tile(shape, I32)
    nc.gpsimd.iota(
        position_int[:],
        pattern=[[GROUP_TOKENS, GROUPS_PER_BATCH], [1, GROUP_TILES]],
        base=0,
        channel_multiplier=GROUP_TILES,
    )
    position = pool.tile(shape, F32)
    nc.vector.tensor_copy(out=position[:], in_=position_int[:])

    shifted = pool.tile(shape, F32)
    nc.vector.tensor_scalar(
        out=shifted[:], in0=position[:], scalar1=1.0 / math.pi, scalar2=ROUND_MAGIC, op0=ALU.mult, op1=ALU.add
    )
    half_turns = pool.tile(shape, F32)
    nc.vector.tensor_scalar(
        out=half_turns[:], in0=shifted[:], scalar1=ROUND_MAGIC, scalar2=None, op0=ALU.subtract
    )
    odd = pool.tile(shape, I32)
    nc.vector.tensor_scalar(
        out=odd[:], in0=shifted[:].bitcast(I32), scalar1=1, scalar2=None, op0=ALU.bitwise_and
    )
    sign = pool.tile(shape, F32)
    nc.vector.tensor_scalar(out=sign[:], in0=odd[:], scalar1=-2.0, scalar2=1.0, op0=ALU.mult, op1=ALU.add)

    rest_a = pool.tile(shape, F32)
    nc.vector.scalar_tensor_tensor(
        out=rest_a[:], in0=half_turns[:], scalar=-PI_HIGH, in1=position[:], op0=ALU.mult, op1=ALU.add
    )
    rest_b = pool.tile(shape, F32)
    nc.vector.scalar_tensor_tensor(
        out=rest_b[:], in0=half_turns[:], scalar=-PI_MIDDLE, in1=rest_a[:], op0=ALU.mult, op1=ALU.add
    )
    rest = pool.tile(shape, F32)
    nc.vector.scalar_tensor_tensor(
        out=rest[:], in0=half_turns[:], scalar=-PI_LOW, in1=rest_b[:], op0=ALU.mult, op1=ALU.add
    )
    rest_plus = pool.tile(shape, F32)
    nc.vector.tensor_scalar(
        out=rest_plus[:], in0=rest[:], scalar1=HALF_PI_HIGH, scalar2=HALF_PI_LOW, op0=ALU.add, op1=ALU.add
    )

    return rest, rest_plus, sign


def take_sines(nc, pool, rest, rest_plus):
    shape = [P, TABLE_COLUMNS]
    sin_rest = pool.tile(shape, F32)
    nc.scalar.activation(out=sin_rest[:], in_=rest[:], func=ACT.Sin)
    cos_rest = pool.tile(shape, F32)
    nc.scalar.activation(out=cos_rest[:], in_=rest_plus[:], func=ACT.Sin)
    return sin_rest, cos_rest


def make_tables(nc, pool, sin_rest, cos_rest, sign):
    shape = [P, TABLE_COLUMNS]
    cos = pool.tile(shape, F32)
    nc.vector.tensor_tensor(out=cos[:], in0=cos_rest[:], in1=sign[:], op=ALU.mult)
    sin = pool.tile(shape, F32)
    nc.vector.tensor_tensor(out=sin[:], in0=sin_rest[:], in1=sign[:], op=ALU.mult)
    neg_sin = pool.tile(shape, F32)
    nc.vector.tensor_scalar(out=neg_sin[:], in0=sin[:], scalar1=-1.0, scalar2=None, op0=ALU.mult)
    return cos, sin, neg_sin


def make_tangents(nc, pool, cos, sin):
    shape = [P, TABLE_COLUMNS]
    inverse_cos = pool.tile(shape, F32)
    nc.vector.reciprocal(out=inverse_cos[:], in_=cos[:])
    tan = pool.tile(shape, F32)
    nc.vector.tensor_tensor(out=tan[:], in0=sin[:], in1=inverse_cos[:], op=ALU.mult)
    neg_tan = pool.tile(shape, F32)
    nc.vector.tensor_scalar(out=neg_tan[:], in0=tan[:], scalar1=-1.0, scalar2=None, op0=ALU.mult)
    return tan, neg_tan


def tile_attention_pa_t_kernel(tc, x, wq_words, wq_scales, wk_words, wk_scales, out_0, out_1):
    nc = tc.nc
    weights = ((wq_words, wq_scales), (wk_words, wk_scales))
    outputs = (out_0, out_1)

    with ExitStack() as ctx:
        consts = ctx.enter_context(tc.tile_pool(name="consts", bufs=1))
        x_pool = ctx.enter_context(tc.tile_pool(name="x", bufs=GROUPS))
        quant_pool = ctx.enter_context(tc.tile_pool(name="quant", bufs=AHEAD + 2))
        cross_pool = ctx.enter_context(tc.tile_pool(name="cross", bufs=6))
        scaled_pool = ctx.enter_context(tc.tile_pool(name="scaled", bufs=2))
        turned_pool = ctx.enter_context(tc.tile_pool(name="turned", bufs=2))
        rot_pool = ctx.enter_context(tc.tile_pool(name="rot", bufs=6))
        psum_x = ctx.enter_context(tc.psum_pool(name="psum_x", bufs=2))
        psum_mm = ctx.enter_context(tc.psum_pool(name="psum_mm", bufs=6))

        def group_rows(tensor_of_batch, g):
            return tensor_of_batch[g % GROUPS_PER_BATCH]

        x_tiles = []

        def load_x(g, pieces):
            x_group = x_pool.tile([P, GROUP_TILES, CH], BF16)
            by_partition = x[g // GROUPS_PER_BATCH].rearrange("(h p j) c -> h p j c", p=P, j=GROUP_TILES)
            for piece in range(pieces):
                tiles = slice(piece * GROUP_TILES // pieces, (piece + 1) * GROUP_TILES // pieces)
                nc.sync.dma_start(out=x_group[:, tiles, :], in_=group_rows(by_partition, g)[:, tiles, :])
            x_tiles.append(x_group)

        zero_words = consts.tile([P, CH // 2], F32)
        nc.vector.memset(zero_words[:], 0.0)
        zeros = zero_words[:].bitcast(BF16)
        w_words = consts.tile([P, 2, 2 * CH], U8, align_bytes=64)
        w_planes = consts.tile([P, 2, CH], U8, align_bytes=64)
        nc.vector.memset(w_planes[:].bitcast(I32), 0)

        load_x(0, GROUP_BANKS)
        load_x(1, 1)
        for which, (words, scales) in enumerate(weights):
            for quadrant in range(4):
                nc.sync.dma_start(
                    out=w_planes[32 * quadrant : 32 * quadrant + 4, which, :].bitcast(I32),
                    in_=scales[0, 4 * quadrant : 4 * quadrant + 4, :].bitcast(I32),
                )
            nc.sync.dma_start(out=w_words[:, which, :].bitcast(I32), in_=words[0].bitcast(I32))
            if which == 0:
                load_x(AHEAD, 1)
        for g in range(AHEAD + 1, GROUPS):
            load_x(g, 1)

        identity = consts.tile([P, P], F32)
        make_identity(nc, identity[:])

        quantised = {}

        def quantise_group(g):
            x_words = x_tiles[g][:].bitcast(F32)
            grouped = quant_pool.tile([P, GROUP_TOKENS, 4], BF16, align_bytes=64)
            codes = quant_pool.tile([P, GROUP_TOKENS], U32, align_bytes=64)
            plane = quant_pool.tile([P, GROUP_TOKENS], U8, align_bytes=64)
            for bank in range(GROUP_BANKS):
                transposed = psum_x.tile([P, BANK_TILES, 2, P], F32)
                for j in range(BANK_TILES):
                    for u in range(2):
                        nc.tensor.transpose(
                            transposed[:, j, u, :],
                            x_words[:, bank * BANK_TILES + j, u:WORDS:2],
                            identity[:],
                        )
                tokens = slice(bank * BANK_TOKENS, (bank + 1) * BANK_TOKENS)
                scalar_takes_both = g >= AHEAD
                copy_out = nc.scalar.copy if bank == 0 or scalar_takes_both else nc.vector.tensor_copy
                copy_out(
                    out=grouped[:, tokens, :].bitcast(F32).rearrange("p (j m) u -> p j m u", j=BANK_TILES),
                    in_=transposed[:].rearrange("p j u m -> p j m u"),
                )
            for bank in range(GROUP_BANKS):
                tokens = slice(bank * BANK_TOKENS, (bank + 1) * BANK_TOKENS)
                nc.vector.quantize_mx(
                    out=codes[:, tokens].bitcast(FP8X4),
                    scales=plane[:, tokens],
                    in_=grouped[:, tokens, :].rearrange("p m t -> p (m t)"),
                )
            quantised[g] = (codes, plane)

        def project(codes, plane, j, which):
            tokens = slice(j * P, (j + 1) * P)
            acc = psum_mm.tile([P, CH], F32)
            nc.tensor.matmul_mx(
                out=acc[:],
                lhsT=codes[:, tokens].bitcast(FP8X4),
                lhsT_scale=plane[:, tokens],
                rhs=w_words[:, which, :].bitcast(FP4X4),
                rhs_scale=w_planes[:, which, :],
                start=True,
                stop=True,
            )
            return acc

        def rotate_on_gpsimd(acc, t, out_tile):
            scaled = scaled_pool.tile([P, CH], F32)
            nc.vector.tensor_scalar(
                out=scaled[:], in0=acc[:], scalar1=cos[:, t : t + 1], scalar2=None, op0=ALU.mult
            )
            scaled_pairs = scaled[:].rearrange("p (i two) -> p i two", two=2)
            turned = turned_pool.tile([P, 2, PAIRS], F32)
            for plane, factor in ((0, neg_tan), (1, tan)):
                nc.gpsimd.tensor_scalar(
                    out=turned[:, plane, :],
                    in0=scaled_pairs[:, :, 1 - plane],
                    scalar1=factor[:, t : t + 1],
                    scalar2=0.0,
                    op0=ALU.mult,
                    op1=ALU.add,
                )
            nc.gpsimd.tensor_tensor(
                out=out_tile.rearrange("p (i two) -> p i two", two=2),
                in0=scaled_pairs,
                in1=turned[:].rearrange("p two i -> p i two"),
                op=ALU.add,
            )

        def project_and_rotate(g, which):
            codes, plane = quantised[g]
            rotated = rot_pool.tile([P, GROUP_TILES, CH], F32)
            first_t = (g % GROUPS_PER_BATCH) * GROUP_TILES
            by_partition = outputs[which][g // GROUPS_PER_BATCH].rearrange(
                "(half p j) h d -> half p j (h d)", p=P, j=GROUP_TILES
            )
            for j in range(GROUP_TILES):
                t = first_t + j
                acc = project(codes, plane, j, which)
                pairs = acc[:].rearrange("p (i two) -> p i two", two=2)
                if j == 0 and which == 1 and g < GPSIMD_GROUPS:
                    rotate_on_gpsimd(acc, t, rotated[:, j, :])
                    continue
                cross = cross_pool.tile([P, 2, PAIRS], F32)
                nc.scalar.activation(
                    out=cross[:, 0, :], in_=pairs[:, :, 1], func=ACT.Copy, scale=neg_sin[:, t : t + 1]
                )
                nc.scalar.activation(
                    out=cross[:, 1, :], in_=pairs[:, :, 0], func=ACT.Copy, scale=sin[:, t : t + 1]
                )
                nc.vector.scalar_tensor_tensor(
                    out=rotated[:, j, :].rearrange("p (i two) -> p i two", two=2),
                    in0=pairs,
                    scalar=cos[:, t : t + 1],
                    in1=cross[:].rearrange("p two i -> p i two"),
                    op0=ALU.mult,
                    op1=ALU.add,
                )
            first_tiles = 1 if which == 1 and g < GPSIMD_GROUPS else 0
            nc.sync.dma_start(
                out=group_rows(by_partition, g)[:, first_tiles:, :], in_=rotated[:, first_tiles:, :]
            )
            if first_tiles > 0:
                nc.sync.dma_start(
                    out=group_rows(by_partition, g)[:, :first_tiles, :], in_=rotated[:, :first_tiles, :]
                )

        with tc.manual_schedule():
            acc = psum_mm.tile([P, CH], F32)
            for step in range(WARM_UP_MATMULS):
                nc.tensor.matmul(out=acc[:], lhsT=zeros[:, :P], rhs=zeros, start=True, stop=True)
            table_load = consts.tile([P, 1], F32)
            nc.scalar.activation(out=table_load[:], in_=zero_words[:, :1], func=ACT.Sin)
            rest, rest_plus, sign = reduce_positions(nc, consts)
            quantise_group(0)
            sin_rest, cos_rest = take_sines(nc, consts, rest, rest_plus)
            cos, sin, neg_sin = make_tables(nc, consts, sin_rest, cos_rest, sign)
            for g in range(1, AHEAD):
                quantise_group(g)
            tan, neg_tan = make_tangents(nc, consts, cos, sin)
            for g in range(GROUPS):
                project_and_rotate(g, 0)
                if g + AHEAD < GROUPS:
                    quantise_group(g + AHEAD)
                project_and_rotate(g, 1)
